import numpy as np
import ml_dtypes


def mxq(x, axis, fmt="e4m3"):
    dtype, down = {"e4m3": (ml_dtypes.float8_e4m3fn, 7), "e5m2": (ml_dtypes.float8_e5m2, 14)}[fmt]
    v = np.moveaxis(np.asarray(x, np.float32).astype(ml_dtypes.bfloat16).astype(np.float64), axis, -1)
    blocks = v.reshape(v.shape[:-1] + (-1, 32))
    amax = np.abs(blocks).max(-1, keepdims=True)
    byte = np.maximum(np.where(amax > 0, np.frexp(amax)[1] - 1 + 127, 0) - down, 1)
    scale = np.exp2(byte - 127.0)
    codes = (blocks / scale).astype(np.float32).astype(dtype).astype(np.float64)
    return np.moveaxis((codes * scale).reshape(v.shape), -1, axis)


WIDE = False


def mx_kscale(k):
    if not WIDE:
        return np.ones(k)
    levels = np.array([10, -10, 5, -5, 0])
    a = np.random.permutation(np.resize(levels, k // 512 * 4)).reshape(k // 512, 4)
    idx = np.arange(k)
    return np.exp2(a[idx // 512, idx % 128 // 32])


BF16 = ml_dtypes.bfloat16


def bf(x):
    return np.asarray(x, np.float32).astype(BF16)


def f64(x):
    return np.asarray(x).astype(np.float64)


N, M, C, C0, C1 = 128, 8, 128, 8192, 256
EPS = 1e-3


def bn_relu(y, gamma, beta):
    mean = y.mean(axis=(0, 1))
    var = y.var(axis=(0, 1))
    return np.maximum((y - mean) * (1.0 / np.sqrt(var + EPS)) * gamma + beta, 0.0)


def setup_inputs():
    t = mx_kscale(C0)
    r0 = 0.05 * 4.0 ** np.random.random(C0)
    return {"voxel_feats": bf(np.random.standard_normal((N, M, C)) + 0.5 * np.random.standard_normal(C)),
            "W0": bf(np.random.standard_normal((C0, C)) / np.sqrt(C) * r0[:, None]),
            "gamma0": bf((1.0 + 0.1 * np.random.standard_normal(C0)) * t),
            "beta0": bf(0.2 * np.random.standard_normal(C0) * t),
            "W1": bf(np.random.standard_normal((C1, 2 * C0)) * 0.2 / np.sqrt(2 * C0) / np.concatenate([t, t])[None, :]),
            "gamma1": bf(1.0 + 0.1 * np.random.standard_normal(C1)),
            "beta1": bf(0.3 * np.random.standard_normal(C1) - 0.5)}


def reference(voxel_feats, W0, gamma0, beta0, W1, gamma1, beta1):
    y0 = f64(voxel_feats) @ f64(W0).T
    p = bn_relu(y0, f64(gamma0), f64(beta0))
    a = p.max(axis=1)
    w1q = mxq(f64(W1).T, 0, "e4m3")
    y1 = (mxq(p, 2, "e4m3") @ w1q[:C0]) + (mxq(a, 1, "e4m3") @ w1q[C0:])[:, None, :]
    return bn_relu(y1, f64(gamma1), f64(beta1)).max(axis=1)

@@ -1,0 +1,306 @@
+from contextlib import ExitStack
+
+import concourse.mybir as mybir
+from concourse.masks import make_identity
+
+BF16 = mybir.dt.bfloat16
+F32 = mybir.dt.float32
+U32 = mybir.dt.uint32
+U8 = mybir.dt.uint8
+FP8X4 = mybir.dt.float8_e4m3fn_x4
+ALU = mybir.AluOpType
+ACT = mybir.ActivationFunctionType
+AX = mybir.AxisListType
+
+P = 128
+VOXELS = 128
+POINTS = 8
+ROWS = VOXELS * POINTS
+C = 128
+C0 = 8192
+C1 = 256
+EPS = 1e-3
+PACK = 4
+K_PASS = P * PACK
+PASSES = C0 // K_PASS
+CHUNKS = C0 // P
+HALF = ROWS // 2
+GROUP = 2
+GROUPS = PASSES // GROUP
+
+FLOPS = 2 * ROWS * C * C0 + 2 * ROWS * C0 * C1 + 2 * VOXELS * C0 * C1
+
+
+def tile_vfe_k_kernel(tc, voxel_feats, W0, gamma0, beta0, W1, gamma1, beta1, out):
+    nc = tc.nc
+    with ExitStack() as ctx:
+        keep = ctx.enter_context(tc.tile_pool(name="keep", bufs=1))
+        flow = ctx.enter_context(tc.tile_pool(name="flow", bufs=3))
+
+        xT = keep.tile([P, ROWS], BF16)
+        ident_bf = keep.tile([P, P], BF16)
+        ident_f32 = keep.tile([P, P], F32)
+        gb = keep.tile([P, 132], F32)
+        w0T = keep.tile([P, CHUNKS, P], BF16)
+        scale0 = keep.tile([P, CHUNKS], F32)
+        shift0 = keep.tile([P, CHUNKS], F32)
+        w1_codes = keep.tile([P, 2, PASSES, C1], U32, align_bytes=64)
+        w1_scales = keep.tile([P, 2, PASSES, C1], U8, align_bytes=64)
+        p_codes_first = keep.tile([P, PASSES, HALF], U32, align_bytes=64)
+        p_scales_first = keep.tile([P, PASSES, HALF], U8, align_bytes=64)
+        peak_first = keep.tile([P, PASSES, PACK * VOXELS], BF16)
+        a_codes = keep.tile([P, PASSES, VOXELS], U32, align_bytes=64)
+        a_scales = keep.tile([P, PASSES, VOXELS], U8, align_bytes=64)
+        gamma0_t = gb[:, 0:CHUNKS]
+        beta0_t = gb[:, CHUNKS : 2 * CHUNKS]
+        gamma1_t = gb[:, 128:130]
+        beta1_t = gb[:, 130:132]
+
+        def layer0(g, half, psum, codes, scales, peak):
+            planes = flow.tile([P, PACK, HALF], BF16)
+            for t in range(PACK):
+                j = PACK * g + t
+                y0_ps = psum.tile([P, HALF], F32, tag="y0")
+                nc.tensor.matmul(out=y0_ps[:], lhsT=w0T[:, j, :], rhs=xT[:, half * HALF : (half + 1) * HALF], start=True, stop=True)
+                nc.scalar.activation(
+                    out=planes[:, t, :], in_=y0_ps[:], func=ACT.Relu, bias=shift0[:, j : j + 1], scale=scale0[:, j : j + 1]
+                )
+            grouped = flow.tile([P, PACK * HALF], BF16, align_bytes=64)
+            nc.vector.tensor_copy(
+                out=grouped[:].rearrange("p (c i t) -> p c t i", i=4, t=PACK),
+                in_=planes[:].rearrange("p t (c i) -> p c t i", i=4),
+            )
+            nc.vector.quantize_mx(out=codes.bitcast(FP8X4), scales=scales, in_=grouped[:])
+            best2 = flow.tile([P, 2 * PACK * VOXELS], BF16)
+            nc.vector.tensor_tensor(out=best2[:], in0=grouped[:, 0:1024], in1=grouped[:, 1024:2048], op=ALU.max)
+            nc.vector.tensor_tensor(out=peak, in0=best2[:, 0:512], in1=best2[:, 512:1024], op=ALU.max)
+
+        with ExitStack() as first:
+            once = first.enter_context(tc.tile_pool(name="once", bufs=1))
+            stage = first.enter_context(tc.tile_pool(name="stage", bufs=2))
+            loads = first.enter_context(tc.tile_pool(name="loads", bufs=4))
+            psum_y0 = first.enter_context(tc.psum_pool(name="psum_y0", bufs=2))
+            psum_two = first.enter_context(tc.psum_pool(name="psum_two", bufs=2))
+            psum_one = first.enter_context(tc.psum_pool(name="psum_one", bufs=1))
+
+            x_sb = once.tile([P, POINTS, C], BF16)
+            nc.sync.dma_start(out=x_sb[:], in_=voxel_feats)
+            gb_rows = once.tile([P, 2 * P], BF16)
+            nc.vector.memset(gb_rows[:], 0.0)
+            nc.scalar.dma_start(out=gb_rows[0:32, :], in_=gamma0.rearrange("(r w) -> r w", w=2 * P))
+            nc.scalar.dma_start(out=gb_rows[32:64, :], in_=beta0.rearrange("(r w) -> r w", w=2 * P))
+            nc.scalar.dma_start(out=gb_rows[64:65, :], in_=gamma1.rearrange("(r w) -> r w", w=2 * P))
+            nc.scalar.dma_start(out=gb_rows[65:66, :], in_=beta1.rearrange("(r w) -> r w", w=2 * P))
+
+            make_identity(nc, ident_bf[:])
+            make_identity(nc, ident_f32[:])
+            ones_bf = once.tile([P, P], BF16)
+            nc.vector.memset(ones_bf[:], 1.0)
+
+            xt_ps = psum_one.tile([P, POINTS, VOXELS], BF16, tag="w0t")
+            for m in range(POINTS):
+                nc.tensor.transpose(xt_ps[:, m, :], x_sb[:, m, :], ident_bf[:])
+            nc.scalar.copy(out=xT[:], in_=xt_ps[:].rearrange("p m n -> p (m n)"))
+
+            sum_ps = psum_two.tile([P, C], F32, tag="wcov")
+            for m in range(POINTS):
+                nc.tensor.matmul(out=sum_ps[:], lhsT=ones_bf[:], rhs=x_sb[:, m, :], start=(m == 0), stop=(m == POINTS - 1))
+            mu_rows = once.tile([P, C], F32)
+            nc.vector.tensor_scalar(out=mu_rows[:], in0=sum_ps[:], scalar1=1.0 / ROWS, scalar2=None, op0=ALU.mult)
+            xc = once.tile([P, POINTS, C], F32)
+            nc.vector.tensor_tensor(
+                out=xc[:], in0=x_sb[:], in1=mu_rows[:].unsqueeze(1).to_broadcast([P, POINTS, C]), op=ALU.subtract
+            )
+            cov_ps = psum_two.tile([P, C], F32, tag="wcov")
+            for m in range(POINTS):
+                nc.tensor.matmul(out=cov_ps[:], lhsT=xc[:, m, :], rhs=xc[:, m, :], start=(m == 0), stop=(m == POINTS - 1))
+            cov = once.tile([P, C], F32)
+            nc.vector.tensor_scalar(out=cov[:], in0=cov_ps[:], scalar1=1.0 / ROWS, scalar2=None, op0=ALU.mult)
+
+            col_ps = psum_one.tile([P, 2], F32, tag="mean")
+            for m in range(POINTS):
+                nc.tensor.matmul(out=col_ps[:], lhsT=x_sb[:, m, :], rhs=ones_bf[:, 0:2], start=(m == 0), stop=(m == POINTS - 1))
+            mu_pieces = once.tile([P, 4], BF16)
+            nc.vector.memset(mu_pieces[:], 0.0)
+            rest0 = once.tile([P, 1], F32)
+            rest1 = once.tile([P, 1], F32)
+            rest2 = once.tile([P, 1], F32)
+            nc.vector.tensor_scalar(out=rest0[:], in0=col_ps[:, 0:1], scalar1=1.0 / ROWS, scalar2=None, op0=ALU.mult)
+            nc.vector.tensor_copy(out=mu_pieces[:, 0:1], in_=rest0[:])
+            nc.vector.tensor_tensor(out=rest1[:], in0=rest0[:], in1=mu_pieces[:, 0:1], op=ALU.subtract)
+            nc.vector.tensor_copy(out=mu_pieces[:, 1:2], in_=rest1[:])
+            nc.vector.tensor_tensor(out=rest2[:], in0=rest1[:], in1=mu_pieces[:, 1:2], op=ALU.subtract)
+            nc.vector.tensor_copy(out=mu_pieces[:, 2:3], in_=rest2[:])
+
+            gb_ps = psum_two.tile([P, P], F32, tag="w1t")
+            nc.tensor.transpose(gb_ps[:], gb_rows[:].bitcast(F32), ident_f32[:])
+            nc.vector.tensor_copy(out=gb[:], in_=gb_ps[:].bitcast(BF16)[:, 0:132])
+
+            w0_view = W0.rearrange("(a p e) c -> p a (e c)", p=P, e=2)
+            w1_view = W1.rearrange("(n h) k -> n h k", h=2)
+
+            def prepare(group):
+                n_chunks = PACK * GROUP
+                cols = slice(n_chunks * group, n_chunks * (group + 1))
+                w0_raw = loads.tile([P, n_chunks, C], BF16)
+                nc.sync.dma_start(
+                    out=w0_raw[:].rearrange("p (a e) c -> p a (e c)", e=2),
+                    in_=w0_view[:, 2 * GROUP * group : 2 * GROUP * (group + 1), :],
+                )
+                w1_raw = []
+                for part in range(2):
+                    k0 = part * C0 + group * GROUP * K_PASS
+                    raw = loads.tile([P, 2, GROUP * K_PASS], BF16, name="w1_raw%d" % part, tag="w1_raw")
+                    nc.sync.dma_start(out=raw[:], in_=w1_view[:, :, k0 : k0 + GROUP * K_PASS])
+                    w1_raw.append(raw)
+
+                var_g = stage.tile([P, n_chunks], F32)
+                mean_ps = psum_one.tile([P, n_chunks, 4], F32, tag="mean")
+                for i in range(GROUP):
+                    local = slice(PACK * i, PACK * (i + 1))
+                    chunks = slice(n_chunks * group + PACK * i, n_chunks * group + PACK * (i + 1))
+                    w0t_ps = psum_one.tile([P, PACK, P], BF16, tag="w0t")
+                    for t in range(PACK):
+                        nc.tensor.transpose(w0t_ps[:, t, :], w0_raw[:, PACK * i + t, :], ident_bf[:])
+                    nc.scalar.copy(out=w0T[:, chunks, :], in_=w0t_ps[:])
+                    w0T_f32 = stage.tile([P, PACK, P], F32)
+                    nc.gpsimd.tensor_scalar(
+                        out=w0T_f32[:], in0=w0T[:, chunks, :], scalar1=1.0, scalar2=0.0, op0=ALU.mult, op1=ALU.add
+                    )
+                    wcov_ps = psum_two.tile([P, PACK, C], F32, tag="wcov")
+                    for t in range(PACK):
+                        nc.tensor.matmul(out=wcov_ps[:, t, :], lhsT=w0T_f32[:, t, :], rhs=cov[:], start=True, stop=True)
+                        nc.tensor.matmul(
+                            out=mean_ps[:, PACK * i + t, :], lhsT=w0T[:, n_chunks * group + PACK * i + t, :], rhs=mu_pieces[:],
+                            start=True, stop=True,
+                        )
+                    prod = stage.tile([P, PACK, C], F32)
+                    nc.vector.tensor_tensor(out=prod[:], in0=wcov_ps[:], in1=w0_raw[:, local, :], op=ALU.mult)
+                    nc.vector.tensor_reduce(out=var_g[:, local], in_=prod[:], axis=AX.X, op=ALU.add)
+                mean_g = stage.tile([P, n_chunks], F32)
+                nc.vector.tensor_reduce(out=mean_g[:], in_=mean_ps[:], axis=AX.X, op=ALU.add)
+                var_eps = stage.tile([P, n_chunks], F32)
+                nc.vector.tensor_scalar(out=var_eps[:], in0=var_g[:], scalar1=EPS, scalar2=None, op0=ALU.add)
+                std_g = stage.tile([P, n_chunks], F32)
+                nc.scalar.sqrt(out=std_g[:], in_=var_eps[:])
+                rstd_g = stage.tile([P, n_chunks], F32)
+                nc.vector.reciprocal(out=rstd_g[:], in_=std_g[:])
+                nc.vector.tensor_tensor(out=scale0[:, cols], in0=gamma0_t[:, cols], in1=rstd_g[:], op=ALU.mult)
+                mscale_g = stage.tile([P, n_chunks], F32)
+                nc.vector.tensor_tensor(out=mscale_g[:], in0=mean_g[:], in1=scale0[:, cols], op=ALU.mult)
+                nc.vector.tensor_tensor(out=shift0[:, cols], in0=beta0_t[:, cols], in1=mscale_g[:], op=ALU.subtract)
+
+                passes = slice(GROUP * group, GROUP * (group + 1))
+                for part in range(2):
+                    w1_words = w1_raw[part][:].bitcast(F32)
+                    w1_grouped = stage.tile([P, GROUP, PACK * C1], BF16, align_bytes=64)
+                    for i in range(GROUP):
+                        w1t_ps = psum_two.tile([P, 2, 2, P], F32, tag="w1t")
+                        for h in range(2):
+                            for u in range(2):
+                                w_lo = 256 * i + 128 * u
+                                nc.tensor.transpose(w1t_ps[:, h, u, :], w1_words[:, h, w_lo : w_lo + 128], ident_f32[:])
+                        nc.scalar.copy(
+                            out=w1_grouped[:, i, :].bitcast(F32).rearrange("p (h n u) -> p h n u", h=2, u=2),
+                            in_=w1t_ps[:].rearrange("p h u n -> p h n u"),
+                        )
+                    nc.vector.quantize_mx(
+                        out=w1_codes[:, part, passes, :].rearrange("p g n -> p (g n)").bitcast(FP8X4),
+                        scales=w1_scales[:, part, passes, :].rearrange("p g n -> p (g n)"),
+                        in_=w1_grouped[:].rearrange("p i w -> p (i w)"),
+                    )
+
+            for step in range(GROUPS + 1):
+                if step < GROUPS:
+                    prepare(step)
+                if step >= 1:
+                    for g in range(GROUP * (step - 1), GROUP * step):
+                        layer0(g, 0, psum_y0, p_codes_first[:, g, :], p_scales_first[:, g, :], peak_first[:, g, :])
+
+        last = ctx.enter_context(tc.tile_pool(name="last", bufs=1))
+        late = ctx.enter_context(tc.tile_pool(name="late", bufs=3))
+        psum_acc = ctx.enter_context(tc.psum_pool(name="psum_acc", bufs=1))
+        psum_rest = ctx.enter_context(tc.psum_pool(name="psum_rest", bufs=4))
+        acc = [[psum_acc.tile([P, HALF], F32, name="acc%d%d" % (h, half)) for half in range(2)] for h in range(2)]
+
+        def layer1(g, half, codes, scales):
+            for h in range(2):
+                nc.tensor.matmul_mx(
+                    out=acc[h][half][:],
+                    lhsT=w1_codes[:, 0, g, h * P : (h + 1) * P].bitcast(FP8X4),
+                    lhsT_scale=w1_scales[:, 0, g, h * P : (h + 1) * P],
+                    rhs=codes.bitcast(FP8X4),
+                    rhs_scale=scales,
+                    start=(g == 0),
+                    stop=(g == PASSES - 1),
+                )
+
+        for g in range(PASSES):
+            p_codes = late.tile([P, HALF], U32, align_bytes=64)
+            p_scales = late.tile([P, HALF], U8, align_bytes=64)
+            peak = late.tile([P, PACK * VOXELS], BF16)
+            layer0(g, 1, psum_rest, p_codes[:], p_scales[:], peak[:])
+            a_grouped = late.tile([P, PACK * VOXELS], BF16, align_bytes=64)
+            nc.vector.tensor_tensor(out=a_grouped[:], in0=peak[:], in1=peak_first[:, g, :], op=ALU.max)
+            nc.vector.quantize_mx(out=a_codes[:, g, :].bitcast(FP8X4), scales=a_scales[:, g, :], in_=a_grouped[:])
+            layer1(g, 0, p_codes_first[:, g, :], p_scales_first[:, g, :])
+            layer1(g, 1, p_codes[:], p_scales[:])
+
+        ya = last.tile([P, 2, VOXELS], F32)
+        for h in range(2):
+            ya_ps = psum_rest.tile([P, VOXELS], F32, tag="y0")
+            for g in range(PASSES):
+                nc.tensor.matmul_mx(
+                    out=ya_ps[:],
+                    lhsT=w1_codes[:, 1, g, h * P : (h + 1) * P].bitcast(FP8X4),
+                    lhsT_scale=w1_scales[:, 1, g, h * P : (h + 1) * P],
+                    rhs=a_codes[:, g, :].bitcast(FP8X4),
+                    rhs_scale=a_scales[:, g, :],
+                    start=(g == 0),
+                    stop=(g == PASSES - 1),
+                )
+            nc.scalar.copy(out=ya[:, h, :], in_=ya_ps[:])
+
+        y1 = last.tile([P, 2, 2, HALF], F32)
+        stats1 = last.tile([P, 2, 2, 6], F32)
+        mv1 = last.tile([P, 2, 2], F32)
+        for h in range(2):
+            for half in range(2):
+                nc.vector.tensor_tensor(
+                    out=y1[:, h, half, :].rearrange("p (m n) -> p m n", n=VOXELS),
+                    in0=acc[h][half][:].rearrange("p (m n) -> p m n", n=VOXELS),
+                    in1=ya[:, h, :].unsqueeze(1).to_broadcast([P, POINTS // 2, VOXELS]),
+                    op=ALU.add,
+                )
+                nc.vector.bn_stats(out=stats1[:, h, half, :], in_=y1[:, h, half, :])
+            nc.vector.bn_aggr(out=mv1[:, h, :], in_=stats1[:, h, :, :].rearrange("p q s -> p (q s)"))
+        var_eps1 = last.tile([P, 2], F32)
+        std1 = last.tile([P, 2], F32)
+        rstd1 = last.tile([P, 2], F32)
+        scale1 = last.tile([P, 2], F32)
+        mscale1 = last.tile([P, 2], F32)
+        shift1 = last.tile([P, 2], F32)
+        nc.vector.tensor_scalar(out=var_eps1[:], in0=mv1[:, :, 1], scalar1=EPS, scalar2=None, op0=ALU.add)
+        nc.scalar.sqrt(out=std1[:], in_=var_eps1[:])
+        nc.vector.reciprocal(out=rstd1[:], in_=std1[:])
+        nc.vector.tensor_tensor(out=scale1[:], in0=gamma1_t, in1=rstd1[:], op=ALU.mult)
+        nc.vector.tensor_tensor(out=mscale1[:], in0=mv1[:, :, 0], in1=scale1[:], op=ALU.mult)
+        nc.vector.tensor_tensor(out=shift1[:], in0=beta1_t, in1=mscale1[:], op=ALU.subtract)
+
+        z = last.tile([P, 2, ROWS], F32)
+        z4 = last.tile([P, 2, 512], F32)
+        z2 = last.tile([P, 2, 256], F32)
+        z1 = last.tile([P, 2, VOXELS], F32)
+        out_ps = psum_rest.tile([P, 2, P], F32, tag="y0")
+        for h in range(2):
+            nc.scalar.activation(
+                out=z[:, h, :], in_=y1[:, h, :, :].rearrange("p q r -> p (q r)"), func=ACT.Relu,
+                bias=shift1[:, h : h + 1], scale=scale1[:, h : h + 1],
+            )
+            nc.vector.tensor_tensor(out=z4[:, h, :], in0=z[:, h, 0:512], in1=z[:, h, 512:1024], op=ALU.max)
+            nc.vector.tensor_tensor(out=z2[:, h, :], in0=z4[:, h, 0:256], in1=z4[:, h, 256:512], op=ALU.max)
+            nc.vector.tensor_tensor(out=z1[:, h, :], in0=z2[:, h, 0:128], in1=z2[:, h, 128:256], op=ALU.max)
+            nc.tensor.transpose(out_ps[:, h, :], z1[:, h, :], ident_f32[:])
+        out_sb = last.tile([P, P, 2], F32)
+        nc.vector.tensor_copy(out=out_sb[:], in_=out_ps[:].rearrange("p h c -> p c h"))
+        nc.sync.dma_start(out=out, in_=out_sb[:].rearrange("p c h -> p (c h)"))

@@ -36,6 +36,8 @@ def tile_vfe_k_kernel(tc, voxel_feats, W0, gamma0, beta0, W1, gamma1, beta1, out
     with ExitStack() as ctx:
         keep = ctx.enter_context(tc.tile_pool(name="keep", bufs=1))
         flow = ctx.enter_context(tc.tile_pool(name="flow", bufs=3))
+        pairs = ctx.enter_context(tc.tile_pool(name="pairs", bufs=2))
+        psum_y0 = ctx.enter_context(tc.psum_pool(name="psum_y0", bufs=4))
 
         xT = keep.tile([P, ROWS], BF16)
         ident_bf = keep.tile([P, P], BF16)
@@ -56,30 +58,30 @@ def tile_vfe_k_kernel(tc, voxel_feats, W0, gamma0, beta0, W1, gamma1, beta1, out
         gamma1_t = gb[:, 128:130]
         beta1_t = gb[:, 130:132]
 
-        def layer0(g, half, psum, codes, scales, peak):
+        def layer0(g, half, grouped, codes, scales):
             planes = flow.tile([P, PACK, HALF], BF16)
             for t in range(PACK):
                 j = PACK * g + t
-                y0_ps = psum.tile([P, HALF], F32, tag="y0")
+                y0_ps = psum_y0.tile([P, HALF], F32, tag="y0")
                 nc.tensor.matmul(out=y0_ps[:], lhsT=w0T[:, j, :], rhs=xT[:, half * HALF : (half + 1) * HALF], start=True, stop=True)
                 nc.scalar.activation(
                     out=planes[:, t, :], in_=y0_ps[:], func=ACT.Relu, bias=shift0[:, j : j + 1], scale=scale0[:, j : j + 1]
                 )
-            grouped = flow.tile([P, PACK * HALF], BF16, align_bytes=64)
             nc.vector.tensor_copy(
-                out=grouped[:].rearrange("p (c i t) -> p c t i", i=4, t=PACK),
+                out=grouped.rearrange("p (c i t) -> p c t i", i=4, t=PACK),
                 in_=planes[:].rearrange("p t (c i) -> p c t i", i=4),
             )
-            nc.vector.quantize_mx(out=codes.bitcast(FP8X4), scales=scales, in_=grouped[:])
-            best2 = flow.tile([P, 2 * PACK * VOXELS], BF16)
-            nc.vector.tensor_tensor(out=best2[:], in0=grouped[:, 0:1024], in1=grouped[:, 1024:2048], op=ALU.max)
-            nc.vector.tensor_tensor(out=peak, in0=best2[:, 0:512], in1=best2[:, 512:1024], op=ALU.max)
+            nc.vector.quantize_mx(out=codes.bitcast(FP8X4), scales=scales, in_=grouped)
+
+        def peak_of_4_points(grouped, peak):
+            best2 = pairs.tile([P, GROUP, 2 * PACK * VOXELS], BF16)
+            nc.vector.tensor_tensor(out=best2[:], in0=grouped[:, :, 0:1024], in1=grouped[:, :, 1024:2048], op=ALU.max)
+            nc.vector.tensor_tensor(out=peak, in0=best2[:, :, 0:512], in1=best2[:, :, 512:1024], op=ALU.max)
 
         with ExitStack() as first:
             once = first.enter_context(tc.tile_pool(name="once", bufs=1))
             stage = first.enter_context(tc.tile_pool(name="stage", bufs=2))
             loads = first.enter_context(tc.tile_pool(name="loads", bufs=4))
-            psum_y0 = first.enter_context(tc.psum_pool(name="psum_y0", bufs=2))
             psum_two = first.enter_context(tc.psum_pool(name="psum_two", bufs=2))
             psum_one = first.enter_context(tc.psum_pool(name="psum_one", bufs=1))
 
@@ -96,11 +98,9 @@ def tile_vfe_k_kernel(tc, voxel_feats, W0, gamma0, beta0, W1, gamma1, beta1, out
             make_identity(nc, ident_f32[:])
             ones_bf = once.tile([P, P], BF16)
             nc.vector.memset(ones_bf[:], 1.0)
-
-            xt_ps = psum_one.tile([P, POINTS, VOXELS], BF16, tag="w0t")
-            for m in range(POINTS):
-                nc.tensor.transpose(xt_ps[:, m, :], x_sb[:, m, :], ident_bf[:])
-            nc.scalar.copy(out=xT[:], in_=xt_ps[:].rearrange("p m n -> p (m n)"))
+            warm = once.tile([P, 1], F32)
+            nc.vector.memset(warm[:], 1.0)
+            nc.scalar.sqrt(out=warm[:], in_=warm[:])
 
             sum_ps = psum_two.tile([P, C], F32, tag="wcov")
             for m in range(POINTS):
@@ -132,27 +132,26 @@ def tile_vfe_k_kernel(tc, voxel_feats, W0, gamma0, beta0, W1, gamma1, beta1, out
             nc.vector.tensor_tensor(out=rest2[:], in0=rest1[:], in1=mu_pieces[:, 1:2], op=ALU.subtract)
             nc.vector.tensor_copy(out=mu_pieces[:, 2:3], in_=rest2[:])
 
-            gb_ps = psum_two.tile([P, P], F32, tag="w1t")
+            xt_ps = psum_one.tile([P, POINTS, VOXELS], BF16, tag="w0t")
+            for m in range(POINTS):
+                nc.tensor.transpose(xt_ps[:, m, :], x_sb[:, m, :], ident_bf[:])
+            nc.scalar.copy(out=xT[:], in_=xt_ps[:].rearrange("p m n -> p (m n)"))
+
+            gb_ps = psum_y0.tile([P, P], F32, tag="y0")
             nc.tensor.transpose(gb_ps[:], gb_rows[:].bitcast(F32), ident_f32[:])
             nc.vector.tensor_copy(out=gb[:], in_=gb_ps[:].bitcast(BF16)[:, 0:132])
 
             w0_view = W0.rearrange("(a p e) c -> p a (e c)", p=P, e=2)
             w1_view = W1.rearrange("(n h) k -> n h k", h=2)
 
-            def prepare(group):
+            def prepare_w0(group):
                 n_chunks = PACK * GROUP
                 cols = slice(n_chunks * group, n_chunks * (group + 1))
                 w0_raw = loads.tile([P, n_chunks, C], BF16)
-                nc.sync.dma_start(
+                nc.scalar.dma_start(
                     out=w0_raw[:].rearrange("p (a e) c -> p a (e c)", e=2),
                     in_=w0_view[:, 2 * GROUP * group : 2 * GROUP * (group + 1), :],
                 )
-                w1_raw = []
-                for part in range(2):
-                    k0 = part * C0 + group * GROUP * K_PASS
-                    raw = loads.tile([P, 2, GROUP * K_PASS], BF16, name="w1_raw%d" % part, tag="w1_raw")
-                    nc.sync.dma_start(out=raw[:], in_=w1_view[:, :, k0 : k0 + GROUP * K_PASS])
-                    w1_raw.append(raw)
 
                 var_g = stage.tile([P, n_chunks], F32)
                 mean_ps = psum_one.tile([P, n_chunks, 4], F32, tag="mean")
@@ -190,12 +189,16 @@ def tile_vfe_k_kernel(tc, voxel_feats, W0, gamma0, beta0, W1, gamma1, beta1, out
                 nc.vector.tensor_tensor(out=mscale_g[:], in0=mean_g[:], in1=scale0[:, cols], op=ALU.mult)
                 nc.vector.tensor_tensor(out=shift0[:, cols], in0=beta0_t[:, cols], in1=mscale_g[:], op=ALU.subtract)
 
+            def prepare_w1(group):
                 passes = slice(GROUP * group, GROUP * (group + 1))
                 for part in range(2):
-                    w1_words = w1_raw[part][:].bitcast(F32)
+                    k0 = part * C0 + group * GROUP * K_PASS
+                    w1_raw = loads.tile([P, 2, GROUP * K_PASS], BF16)
+                    nc.sync.dma_start(out=w1_raw[:], in_=w1_view[:, :, k0 : k0 + GROUP * K_PASS])
+                    w1_words = w1_raw[:].bitcast(F32)
                     w1_grouped = stage.tile([P, GROUP, PACK * C1], BF16, align_bytes=64)
                     for i in range(GROUP):
-                        w1t_ps = psum_two.tile([P, 2, 2, P], F32, tag="w1t")
+                        w1t_ps = psum_y0.tile([P, 2, 2, P], F32, tag="y0")
                         for h in range(2):
                             for u in range(2):
                                 w_lo = 256 * i + 128 * u
@@ -210,17 +213,22 @@ def tile_vfe_k_kernel(tc, voxel_feats, W0, gamma0, beta0, W1, gamma1, beta1, out
                         in_=w1_grouped[:].rearrange("p i w -> p (i w)"),
                     )
 
-            for step in range(GROUPS + 1):
+            prepare_w0(0)
+            for group in range(GROUPS):
+                prepare_w1(group)
+            for step in range(1, GROUPS + 1):
                 if step < GROUPS:
-                    prepare(step)
-                if step >= 1:
-                    for g in range(GROUP * (step - 1), GROUP * step):
-                        layer0(g, 0, psum_y0, p_codes_first[:, g, :], p_scales_first[:, g, :], peak_first[:, g, :])
+                    prepare_w0(step)
+                passes = slice(GROUP * (step - 1), GROUP * step)
+                grouped = pairs.tile([P, GROUP, PACK * HALF], BF16, align_bytes=64)
+                for i in range(GROUP):
+                    g = GROUP * (step - 1) + i
+                    layer0(g, 0, grouped[:, i, :], p_codes_first[:, g, :], p_scales_first[:, g, :])
+                peak_of_4_points(grouped, peak_first[:, passes, :])
 
         last = ctx.enter_context(tc.tile_pool(name="last", bufs=1))
         late = ctx.enter_context(tc.tile_pool(name="late", bufs=3))
         psum_acc = ctx.enter_context(tc.psum_pool(name="psum_acc", bufs=1))
-        psum_rest = ctx.enter_context(tc.psum_pool(name="psum_rest", bufs=4))
         acc = [[psum_acc.tile([P, HALF], F32, name="acc%d%d" % (h, half)) for half in range(2)] for h in range(2)]
 
         def layer1(g, half, codes, scales):
@@ -235,20 +243,29 @@ def tile_vfe_k_kernel(tc, voxel_feats, W0, gamma0, beta0, W1, gamma1, beta1, out
                     stop=(g == PASSES - 1),
                 )
 
-        for g in range(PASSES):
-            p_codes = late.tile([P, HALF], U32, align_bytes=64)
-            p_scales = late.tile([P, HALF], U8, align_bytes=64)
-            peak = late.tile([P, PACK * VOXELS], BF16)
-            layer0(g, 1, psum_rest, p_codes[:], p_scales[:], peak[:])
-            a_grouped = late.tile([P, PACK * VOXELS], BF16, align_bytes=64)
-            nc.vector.tensor_tensor(out=a_grouped[:], in0=peak[:], in1=peak_first[:, g, :], op=ALU.max)
-            nc.vector.quantize_mx(out=a_codes[:, g, :].bitcast(FP8X4), scales=a_scales[:, g, :], in_=a_grouped[:])
-            layer1(g, 0, p_codes_first[:, g, :], p_scales_first[:, g, :])
-            layer1(g, 1, p_codes[:], p_scales[:])
+        for group in range(GROUPS):
+            passes = slice(GROUP * group, GROUP * (group + 1))
+            grouped = pairs.tile([P, GROUP, PACK * HALF], BF16, align_bytes=64)
+            for i in range(GROUP):
+                g = GROUP * group + i
+                p_codes = late.tile([P, HALF], U32, align_bytes=64)
+                p_scales = late.tile([P, HALF], U8, align_bytes=64)
+                layer0(g, 1, grouped[:, i, :], p_codes[:], p_scales[:])
+                layer1(g, 0, p_codes_first[:, g, :], p_scales_first[:, g, :])
+                layer1(g, 1, p_codes[:], p_scales[:])
+            peak = late.tile([P, GROUP, PACK * VOXELS], BF16)
+            peak_of_4_points(grouped, peak[:])
+            a_grouped = late.tile([P, GROUP, PACK * VOXELS], BF16, align_bytes=64)
+            nc.vector.tensor_tensor(out=a_grouped[:], in0=peak[:], in1=peak_first[:, passes, :], op=ALU.max)
+            nc.vector.quantize_mx(
+                out=a_codes[:, passes, :].rearrange("p g n -> p (g n)").bitcast(FP8X4),
+                scales=a_scales[:, passes, :].rearrange("p g n -> p (g n)"),
+                in_=a_grouped[:].rearrange("p g w -> p (g w)"),
+            )
 
         ya = last.tile([P, 2, VOXELS], F32)
         for h in range(2):
-            ya_ps = psum_rest.tile([P, VOXELS], F32, tag="y0")
+            ya_ps = psum_y0.tile([P, VOXELS], F32, tag="y0")
             for g in range(PASSES):
                 nc.tensor.matmul_mx(
                     out=ya_ps[:],
@@ -291,7 +308,7 @@ def tile_vfe_k_kernel(tc, voxel_feats, W0, gamma0, beta0, W1, gamma1, beta1, out
         z4 = last.tile([P, 2, 512], F32)
         z2 = last.tile([P, 2, 256], F32)
         z1 = last.tile([P, 2, VOXELS], F32)
-        out_ps = psum_rest.tile([P, 2, P], F32, tag="y0")
+        out_ps = psum_y0.tile([P, 2, P], F32, tag="y0")
         for h in range(2):
             nc.scalar.activation(
                 out=z[:, h, :], in_=y1[:, h, :, :].rearrange("p q r -> p (q r)"), func=ACT.Relu,

@@ -25,8 +25,12 @@ K_PASS = P * PACK
 PASSES = C0 // K_PASS
 CHUNKS = C0 // P
 HALF = ROWS // 2
-GROUP = 2
-GROUPS = PASSES // GROUP
+UNITS = 2 * PASSES
+LEAD_W0 = 4
+LEAD_VAR = 3
+LEAD_BN = 2
+LEAD_W1 = 4
+FETCH = 2
 
 FLOPS = 2 * ROWS * C * C0 + 2 * ROWS * C0 * C1 + 2 * VOXELS * C0 * C1
 
@@ -34,10 +38,10 @@ FLOPS = 2 * ROWS * C * C0 + 2 * ROWS * C0 * C1 + 2 * VOXELS * C0 * C1
 def tile_vfe_k_kernel(tc, voxel_feats, W0, gamma0, beta0, W1, gamma1, beta1, out):
     nc = tc.nc
     with ExitStack() as ctx:
+        ctx.enter_context(tc.manual_schedule())
         keep = ctx.enter_context(tc.tile_pool(name="keep", bufs=1))
         flow = ctx.enter_context(tc.tile_pool(name="flow", bufs=3))
-        pairs = ctx.enter_context(tc.tile_pool(name="pairs", bufs=2))
-        psum_y0 = ctx.enter_context(tc.psum_pool(name="psum_y0", bufs=4))
+        psum_y0 = ctx.enter_context(tc.psum_pool(name="psum_y0", bufs=3))
 
         xT = keep.tile([P, ROWS], BF16)
         ident_bf = keep.tile([P, P], BF16)
@@ -46,8 +50,8 @@ def tile_vfe_k_kernel(tc, voxel_feats, W0, gamma0, beta0, W1, gamma1, beta1, out
         w0T = keep.tile([P, CHUNKS, P], BF16)
         scale0 = keep.tile([P, CHUNKS], F32)
         shift0 = keep.tile([P, CHUNKS], F32)
-        w1_codes = keep.tile([P, 2, PASSES, C1], U32, align_bytes=64)
-        w1_scales = keep.tile([P, 2, PASSES, C1], U8, align_bytes=64)
+        w1_codes = keep.tile([P, PASSES, 2, C1], U32, align_bytes=64)
+        w1_scales = keep.tile([P, PASSES, 2, C1], U8, align_bytes=64)
         p_codes_first = keep.tile([P, PASSES, HALF], U32, align_bytes=64)
         p_scales_first = keep.tile([P, PASSES, HALF], U8, align_bytes=64)
         peak_first = keep.tile([P, PASSES, PACK * VOXELS], BF16)
@@ -58,25 +62,52 @@ def tile_vfe_k_kernel(tc, voxel_feats, W0, gamma0, beta0, W1, gamma1, beta1, out
         gamma1_t = gb[:, 128:130]
         beta1_t = gb[:, 130:132]
 
-        def layer0(g, half, grouped, codes, scales):
-            planes = flow.tile([P, PACK, HALF], BF16)
+        planes = {}
+        grouped = {}
+        best2 = {}
+        p_codes = {}
+        p_scales = {}
+        peak = {}
+
+        def matmul_and_relu(u):
+            g, sweep = u % PASSES, u // PASSES
+            planes[u] = flow.tile([P, PACK, HALF], BF16, name="planes")
             for t in range(PACK):
                 j = PACK * g + t
                 y0_ps = psum_y0.tile([P, HALF], F32, tag="y0")
-                nc.tensor.matmul(out=y0_ps[:], lhsT=w0T[:, j, :], rhs=xT[:, half * HALF : (half + 1) * HALF], start=True, stop=True)
+                nc.tensor.matmul(out=y0_ps[:], lhsT=w0T[:, j, :], rhs=xT[:, sweep * HALF : (sweep + 1) * HALF], start=True, stop=True)
                 nc.scalar.activation(
-                    out=planes[:, t, :], in_=y0_ps[:], func=ACT.Relu, bias=shift0[:, j : j + 1], scale=scale0[:, j : j + 1]
+                    out=planes[u][:, t, :], in_=y0_ps[:], func=ACT.Relu, bias=shift0[:, j : j + 1], scale=scale0[:, j : j + 1]
                 )
-            nc.vector.tensor_copy(
-                out=grouped.rearrange("p (c i t) -> p c t i", i=4, t=PACK),
-                in_=planes[:].rearrange("p t (c i) -> p c t i", i=4),
-            )
-            nc.vector.quantize_mx(out=codes.bitcast(FP8X4), scales=scales, in_=grouped)
 
-        def peak_of_4_points(grouped, peak):
-            best2 = pairs.tile([P, GROUP, 2 * PACK * VOXELS], BF16)
-            nc.vector.tensor_tensor(out=best2[:], in0=grouped[:, :, 0:1024], in1=grouped[:, :, 1024:2048], op=ALU.max)
-            nc.vector.tensor_tensor(out=peak, in0=best2[:, :, 0:512], in1=best2[:, :, 512:1024], op=ALU.max)
+        def regroup(u):
+            grouped[u] = flow.tile([P, PACK * HALF], BF16, name="grouped", align_bytes=64)
+            nc.vector.tensor_copy(
+                out=grouped[u][:].rearrange("p (c i t) -> p c t i", i=4, t=PACK),
+                in_=planes[u][:].rearrange("p t (c i) -> p c t i", i=4),
+            )
+
+        def quantise_p(u):
+            g, sweep = u % PASSES, u // PASSES
+            if sweep == 0:
+                p_codes[u] = p_codes_first[:, g, :]
+                p_scales[u] = p_scales_first[:, g, :]
+            else:
+                p_codes[u] = late.tile([P, HALF], U32, name="p_codes", align_bytes=64)[:]
+                p_scales[u] = late.tile([P, HALF], U8, name="p_scales", align_bytes=64)[:]
+            nc.vector.quantize_mx(out=p_codes[u].bitcast(FP8X4), scales=p_scales[u], in_=grouped[u][:])
+
+        def best_of_2_pairs(u):
+            best2[u] = flow.tile([P, 2 * PACK * VOXELS], BF16, name="best2")
+            nc.vector.tensor_tensor(out=best2[u][:], in0=grouped[u][:, 0:1024], in1=grouped[u][:, 1024:2048], op=ALU.max)
+
+        def best_of_4_points(u):
+            g, sweep = u % PASSES, u // PASSES
+            if sweep == 0:
+                peak[u] = peak_first[:, g, :]
+            else:
+                peak[u] = late.tile([P, PACK * VOXELS], BF16, name="peak")[:]
+            nc.vector.tensor_tensor(out=peak[u], in0=best2[u][:, 0:512], in1=best2[u][:, 512:1024], op=ALU.max)
 
         with ExitStack() as first:
             once = first.enter_context(tc.tile_pool(name="once", bufs=1))
@@ -93,33 +124,56 @@ def tile_vfe_k_kernel(tc, voxel_feats, W0, gamma0, beta0, W1, gamma1, beta1, out
             nc.scalar.dma_start(out=gb_rows[32:64, :], in_=beta0.rearrange("(r w) -> r w", w=2 * P))
             nc.scalar.dma_start(out=gb_rows[64:65, :], in_=gamma1.rearrange("(r w) -> r w", w=2 * P))
             nc.scalar.dma_start(out=gb_rows[65:66, :], in_=beta1.rearrange("(r w) -> r w", w=2 * P))
+            w0_sb = once.tile([P, CHUNKS, C], BF16)
+            w0_view = W0.rearrange("(a p e) c -> p a (e c)", p=P, e=2)
+            w0_dst = w0_sb[:].rearrange("p (a e) c -> p a (e c)", e=2)
+            for piece in range(4):
+                rows = slice(8 * piece, 8 * piece + 8)
+                nc.scalar.dma_start(out=w0_dst[:, rows, :], in_=w0_view[:, rows, :])
+            w1_view = W1.rearrange("(n h) k -> n h k", h=2)
+            w1_raw = {}
+
+            def load_w1(g):
+                w1_raw[g] = loads.tile([P, 2, 2, K_PASS], BF16, name="w1_raw")
+                for part in range(2):
+                    k0 = part * C0 + g * K_PASS
+                    nc.sync.dma_start(out=w1_raw[g][:, part, :, :], in_=w1_view[:, :, k0 : k0 + K_PASS])
+
+            for g in range(FETCH):
+                load_w1(g)
 
             make_identity(nc, ident_bf[:])
             make_identity(nc, ident_f32[:])
             ones_bf = once.tile([P, P], BF16)
             nc.vector.memset(ones_bf[:], 1.0)
+            eps_col = once.tile([P, 1], F32)
+            nc.vector.memset(eps_col[:], 0.0)
+            nc.vector.tensor_scalar(out=eps_col[:], in0=eps_col[:], scalar1=EPS, scalar2=None, op0=ALU.add)
             warm = once.tile([P, 1], F32)
-            nc.vector.memset(warm[:], 1.0)
-            nc.scalar.sqrt(out=warm[:], in_=warm[:])
+            nc.scalar.sqrt(out=warm[:], in_=eps_col[:])
 
             sum_ps = psum_two.tile([P, C], F32, tag="wcov")
             for m in range(POINTS):
                 nc.tensor.matmul(out=sum_ps[:], lhsT=ones_bf[:], rhs=x_sb[:, m, :], start=(m == 0), stop=(m == POINTS - 1))
+            col_ps = psum_one.tile([P, 2], F32, tag="mean")
+            for m in range(POINTS):
+                nc.tensor.matmul(out=col_ps[:], lhsT=x_sb[:, m, :], rhs=ones_bf[:, 0:2], start=(m == 0), stop=(m == POINTS - 1))
             mu_rows = once.tile([P, C], F32)
             nc.vector.tensor_scalar(out=mu_rows[:], in0=sum_ps[:], scalar1=1.0 / ROWS, scalar2=None, op0=ALU.mult)
             xc = once.tile([P, POINTS, C], F32)
             nc.vector.tensor_tensor(
                 out=xc[:], in0=x_sb[:], in1=mu_rows[:].unsqueeze(1).to_broadcast([P, POINTS, C]), op=ALU.subtract
             )
+            xt_ps = psum_one.tile([P, POINTS, VOXELS], BF16, tag="w0t")
+            for m in range(POINTS):
+                nc.tensor.transpose(xt_ps[:, m, :], x_sb[:, m, :], ident_bf[:])
+            nc.scalar.copy(out=xT[:], in_=xt_ps[:].rearrange("p m n -> p (m n)"))
+            gb_ps = psum_one.tile([P, P], F32, tag="w1t")
+            nc.tensor.transpose(gb_ps[:], gb_rows[:].bitcast(F32), ident_f32[:])
             cov_ps = psum_two.tile([P, C], F32, tag="wcov")
             for m in range(POINTS):
                 nc.tensor.matmul(out=cov_ps[:], lhsT=xc[:, m, :], rhs=xc[:, m, :], start=(m == 0), stop=(m == POINTS - 1))
-            cov = once.tile([P, C], F32)
-            nc.vector.tensor_scalar(out=cov[:], in0=cov_ps[:], scalar1=1.0 / ROWS, scalar2=None, op0=ALU.mult)
 
-            col_ps = psum_one.tile([P, 2], F32, tag="mean")
-            for m in range(POINTS):
-                nc.tensor.matmul(out=col_ps[:], lhsT=x_sb[:, m, :], rhs=ones_bf[:, 0:2], start=(m == 0), stop=(m == POINTS - 1))
             mu_pieces = once.tile([P, 4], BF16)
             nc.vector.memset(mu_pieces[:], 0.0)
             rest0 = once.tile([P, 1], F32)
@@ -131,165 +185,203 @@ def tile_vfe_k_kernel(tc, voxel_feats, W0, gamma0, beta0, W1, gamma1, beta1, out
             nc.vector.tensor_copy(out=mu_pieces[:, 1:2], in_=rest1[:])
             nc.vector.tensor_tensor(out=rest2[:], in0=rest1[:], in1=mu_pieces[:, 1:2], op=ALU.subtract)
             nc.vector.tensor_copy(out=mu_pieces[:, 2:3], in_=rest2[:])
-
-            xt_ps = psum_one.tile([P, POINTS, VOXELS], BF16, tag="w0t")
-            for m in range(POINTS):
-                nc.tensor.transpose(xt_ps[:, m, :], x_sb[:, m, :], ident_bf[:])
-            nc.scalar.copy(out=xT[:], in_=xt_ps[:].rearrange("p m n -> p (m n)"))
-
-            gb_ps = psum_y0.tile([P, P], F32, tag="y0")
-            nc.tensor.transpose(gb_ps[:], gb_rows[:].bitcast(F32), ident_f32[:])
             nc.vector.tensor_copy(out=gb[:], in_=gb_ps[:].bitcast(BF16)[:, 0:132])
+            cov = once.tile([P, C], F32)
+            nc.vector.tensor_scalar(out=cov[:], in0=cov_ps[:], scalar1=1.0 / ROWS, scalar2=None, op0=ALU.mult)
 
-            w0_view = W0.rearrange("(a p e) c -> p a (e c)", p=P, e=2)
-            w1_view = W1.rearrange("(n h) k -> n h k", h=2)
+            var0 = once.tile([P, CHUNKS], F32)
+            std0 = once.tile([P, CHUNKS], F32)
+            rstd0 = once.tile([P, CHUNKS], F32)
+            mean_pieces = once.tile([P, CHUNKS, 4], F32)
+            mean_hi = once.tile([P, CHUNKS], F32)
+            mean0 = once.tile([P, CHUNKS], F32)
+            mscale0 = once.tile([P, CHUNKS], F32)
+            w0T_f32 = {}
+            wcov_ps = {}
+            mean_ps = {}
+            prod = {}
+            w1_grouped = {}
 
-            def prepare_w0(group):
-                n_chunks = PACK * GROUP
-                cols = slice(n_chunks * group, n_chunks * (group + 1))
-                w0_raw = loads.tile([P, n_chunks, C], BF16)
-                nc.scalar.dma_start(
-                    out=w0_raw[:].rearrange("p (a e) c -> p a (e c)", e=2),
-                    in_=w0_view[:, 2 * GROUP * group : 2 * GROUP * (group + 1), :],
+            def transpose_w0(g):
+                chunks = slice(PACK * g, PACK * (g + 1))
+                w0t_ps = psum_one.tile([P, PACK, P], BF16, tag="w0t")
+                for t in range(PACK):
+                    nc.tensor.transpose(w0t_ps[:, t, :], w0_sb[:, PACK * g + t, :], ident_bf[:])
+                nc.scalar.copy(out=w0T[:, chunks, :], in_=w0t_ps[:])
+                w0T_f32[g] = stage.tile([P, PACK, P], F32, name="w0T_f32")
+                nc.gpsimd.tensor_scalar(
+                    out=w0T_f32[g][:], in0=w0T[:, chunks, :], scalar1=1.0, scalar2=0.0, op0=ALU.mult, op1=ALU.add
                 )
 
-                var_g = stage.tile([P, n_chunks], F32)
-                mean_ps = psum_one.tile([P, n_chunks, 4], F32, tag="mean")
-                for i in range(GROUP):
-                    local = slice(PACK * i, PACK * (i + 1))
-                    chunks = slice(n_chunks * group + PACK * i, n_chunks * group + PACK * (i + 1))
-                    w0t_ps = psum_one.tile([P, PACK, P], BF16, tag="w0t")
-                    for t in range(PACK):
-                        nc.tensor.transpose(w0t_ps[:, t, :], w0_raw[:, PACK * i + t, :], ident_bf[:])
-                    nc.scalar.copy(out=w0T[:, chunks, :], in_=w0t_ps[:])
-                    w0T_f32 = stage.tile([P, PACK, P], F32)
-                    nc.gpsimd.tensor_scalar(
-                        out=w0T_f32[:], in0=w0T[:, chunks, :], scalar1=1.0, scalar2=0.0, op0=ALU.mult, op1=ALU.add
-                    )
-                    wcov_ps = psum_two.tile([P, PACK, C], F32, tag="wcov")
-                    for t in range(PACK):
-                        nc.tensor.matmul(out=wcov_ps[:, t, :], lhsT=w0T_f32[:, t, :], rhs=cov[:], start=True, stop=True)
-                        nc.tensor.matmul(
-                            out=mean_ps[:, PACK * i + t, :], lhsT=w0T[:, n_chunks * group + PACK * i + t, :], rhs=mu_pieces[:],
-                            start=True, stop=True,
-                        )
-                    prod = stage.tile([P, PACK, C], F32)
-                    nc.vector.tensor_tensor(out=prod[:], in0=wcov_ps[:], in1=w0_raw[:, local, :], op=ALU.mult)
-                    nc.vector.tensor_reduce(out=var_g[:, local], in_=prod[:], axis=AX.X, op=ALU.add)
-                mean_g = stage.tile([P, n_chunks], F32)
-                nc.vector.tensor_reduce(out=mean_g[:], in_=mean_ps[:], axis=AX.X, op=ALU.add)
-                var_eps = stage.tile([P, n_chunks], F32)
-                nc.vector.tensor_scalar(out=var_eps[:], in0=var_g[:], scalar1=EPS, scalar2=None, op0=ALU.add)
-                std_g = stage.tile([P, n_chunks], F32)
-                nc.scalar.sqrt(out=std_g[:], in_=var_eps[:])
-                rstd_g = stage.tile([P, n_chunks], F32)
-                nc.vector.reciprocal(out=rstd_g[:], in_=std_g[:])
-                nc.vector.tensor_tensor(out=scale0[:, cols], in0=gamma0_t[:, cols], in1=rstd_g[:], op=ALU.mult)
-                mscale_g = stage.tile([P, n_chunks], F32)
-                nc.vector.tensor_tensor(out=mscale_g[:], in0=mean_g[:], in1=scale0[:, cols], op=ALU.mult)
-                nc.vector.tensor_tensor(out=shift0[:, cols], in0=beta0_t[:, cols], in1=mscale_g[:], op=ALU.subtract)
+            def w0_times_cov(g):
+                wcov_ps[g] = psum_two.tile([P, PACK, C], F32, name="wcov_ps", tag="wcov")
+                mean_ps[g] = psum_one.tile([P, PACK, 4], F32, name="mean_ps", tag="mean")
+                for t in range(PACK):
+                    nc.tensor.matmul(out=wcov_ps[g][:, t, :], lhsT=w0T_f32[g][:, t, :], rhs=cov[:], start=True, stop=True)
+                    nc.tensor.matmul(out=mean_ps[g][:, t, :], lhsT=w0T[:, PACK * g + t, :], rhs=mu_pieces[:], start=True, stop=True)
 
-            def prepare_w1(group):
-                passes = slice(GROUP * group, GROUP * (group + 1))
-                for part in range(2):
-                    k0 = part * C0 + group * GROUP * K_PASS
-                    w1_raw = loads.tile([P, 2, GROUP * K_PASS], BF16)
-                    nc.sync.dma_start(out=w1_raw[:], in_=w1_view[:, :, k0 : k0 + GROUP * K_PASS])
-                    w1_words = w1_raw[:].bitcast(F32)
-                    w1_grouped = stage.tile([P, GROUP, PACK * C1], BF16, align_bytes=64)
-                    for i in range(GROUP):
-                        w1t_ps = psum_y0.tile([P, 2, 2, P], F32, tag="y0")
-                        for h in range(2):
-                            for u in range(2):
-                                w_lo = 256 * i + 128 * u
-                                nc.tensor.transpose(w1t_ps[:, h, u, :], w1_words[:, h, w_lo : w_lo + 128], ident_f32[:])
-                        nc.scalar.copy(
-                            out=w1_grouped[:, i, :].bitcast(F32).rearrange("p (h n u) -> p h n u", h=2, u=2),
-                            in_=w1t_ps[:].rearrange("p h u n -> p h n u"),
-                        )
-                    nc.vector.quantize_mx(
-                        out=w1_codes[:, part, passes, :].rearrange("p g n -> p (g n)").bitcast(FP8X4),
-                        scales=w1_scales[:, part, passes, :].rearrange("p g n -> p (g n)"),
-                        in_=w1_grouped[:].rearrange("p i w -> p (i w)"),
-                    )
+            def save_mean(g):
+                nc.scalar.copy(out=mean_pieces[:, PACK * g : PACK * (g + 1), :], in_=mean_ps[g][:])
 
-            prepare_w0(0)
-            for group in range(GROUPS):
-                prepare_w1(group)
-            for step in range(1, GROUPS + 1):
-                if step < GROUPS:
-                    prepare_w0(step)
-                passes = slice(GROUP * (step - 1), GROUP * step)
-                grouped = pairs.tile([P, GROUP, PACK * HALF], BF16, align_bytes=64)
-                for i in range(GROUP):
-                    g = GROUP * (step - 1) + i
-                    layer0(g, 0, grouped[:, i, :], p_codes_first[:, g, :], p_scales_first[:, g, :])
-                peak_of_4_points(grouped, peak_first[:, passes, :])
+            def variance_product(g):
+                prod[g] = stage.tile([P, PACK, C], F32, name="prod")
+                nc.vector.tensor_tensor(out=prod[g][:], in0=wcov_ps[g][:], in1=w0_sb[:, PACK * g : PACK * (g + 1), :], op=ALU.mult)
+
+            def variance_sum(g):
+                nc.vector.tensor_reduce(out=var0[:, PACK * g : PACK * (g + 1)], in_=prod[g][:], axis=AX.X, op=ALU.add)
+
+            def standard_deviation(g):
+                cols = slice(PACK * g, PACK * (g + 1))
+                nc.scalar.activation(out=std0[:, cols], in_=var0[:, cols], func=ACT.Sqrt, bias=eps_col[:, 0:1], scale=1.0)
+
+            def one_over_std(g):
+                cols = slice(PACK * g, PACK * (g + 1))
+                nc.vector.reciprocal(out=rstd0[:, cols], in_=std0[:, cols])
+
+            def scale_and_shift(g):
+                cols = slice(PACK * g, PACK * (g + 1))
+                nc.gpsimd.tensor_tensor(out=mean_hi[:, cols], in0=mean_pieces[:, cols, 0], in1=mean_pieces[:, cols, 1], op=ALU.add)
+                nc.gpsimd.tensor_tensor(out=mean0[:, cols], in0=mean_hi[:, cols], in1=mean_pieces[:, cols, 2], op=ALU.add)
+                nc.gpsimd.tensor_tensor(out=scale0[:, cols], in0=gamma0_t[:, cols], in1=rstd0[:, cols], op=ALU.mult)
+                nc.gpsimd.tensor_tensor(out=mscale0[:, cols], in0=mean0[:, cols], in1=scale0[:, cols], op=ALU.mult)
+                nc.gpsimd.tensor_tensor(out=shift0[:, cols], in0=beta0_t[:, cols], in1=mscale0[:, cols], op=ALU.subtract)
+
+            def transpose_w1(g, part):
+                if part == 0:
+                    w1_grouped[g] = stage.tile([P, 2, PACK * C1], BF16, name="w1_grouped", align_bytes=64)
+                w1_words = w1_raw[g][:, part, :, :].bitcast(F32)
+                w1t_ps = psum_one.tile([P, 2, 2, P], F32, tag="w1t")
+                for h in range(2):
+                    for u in range(2):
+                        nc.tensor.transpose(w1t_ps[:, h, u, :], w1_words[:, h, 128 * u : 128 * (u + 1)], ident_f32[:])
+                nc.scalar.copy(
+                    out=w1_grouped[g][:, part, :].bitcast(F32).rearrange("p (h n u) -> p h n u", h=2, u=2),
+                    in_=w1t_ps[:].rearrange("p h u n -> p h n u"),
+                )
+
+            def quantise_w1(g):
+                nc.vector.quantize_mx(
+                    out=w1_codes[:, g, :, :].rearrange("p s n -> p (s n)").bitcast(FP8X4),
+                    scales=w1_scales[:, g, :, :].rearrange("p s n -> p (s n)"),
+                    in_=w1_grouped[g][:].rearrange("p s w -> p (s w)"),
+                )
+
+            def in_range(g):
+                return 0 <= g < PASSES
+
+            for k in range(-LEAD_W0, PASSES):
+                if in_range(k + LEAD_W1 + FETCH):
+                    load_w1(k + LEAD_W1 + FETCH)
+                if in_range(k + LEAD_W0 - 1):
+                    save_mean(k + LEAD_W0 - 1)
+                if in_range(k + LEAD_BN):
+                    standard_deviation(k + LEAD_BN)
+                if in_range(k + LEAD_W0):
+                    transpose_w0(k + LEAD_W0)
+                if in_range(k + LEAD_W1):
+                    transpose_w1(k + LEAD_W1, 0)
+                if in_range(k):
+                    matmul_and_relu(k)
+                if in_range(k + LEAD_W1):
+                    transpose_w1(k + LEAD_W1, 1)
+                if in_range(k + LEAD_W0):
+                    w0_times_cov(k + LEAD_W0)
+                if in_range(k - 1):
+                    regroup(k - 1)
+                if in_range(k + LEAD_BN):
+                    one_over_std(k + LEAD_BN)
+                    scale_and_shift(k + LEAD_BN)
+                if in_range(k + LEAD_VAR):
+                    variance_product(k + LEAD_VAR)
+                if in_range(k - 2):
+                    best_of_2_pairs(k - 2)
+                if in_range(k - 1):
+                    quantise_p(k - 1)
+                if in_range(k + LEAD_VAR):
+                    variance_sum(k + LEAD_VAR)
+                if in_range(k - 2):
+                    best_of_4_points(k - 2)
+                if in_range(k + LEAD_W1 - 1):
+                    quantise_w1(k + LEAD_W1 - 1)
 
         last = ctx.enter_context(tc.tile_pool(name="last", bufs=1))
-        late = ctx.enter_context(tc.tile_pool(name="late", bufs=3))
+        late = ctx.enter_context(tc.tile_pool(name="late", bufs=4))
         psum_acc = ctx.enter_context(tc.psum_pool(name="psum_acc", bufs=1))
-        acc = [[psum_acc.tile([P, HALF], F32, name="acc%d%d" % (h, half)) for half in range(2)] for h in range(2)]
+        acc = [[psum_acc.tile([P, HALF], F32, name="acc%d%d" % (h, sweep)) for sweep in range(2)] for h in range(2)]
+        a_grouped = {}
 
-        def layer1(g, half, codes, scales):
+        def layer1(g):
+            for sweep in range(2):
+                for h in range(2):
+                    nc.tensor.matmul_mx(
+                        out=acc[h][sweep][:],
+                        lhsT=w1_codes[:, g, 0, h * P : (h + 1) * P].bitcast(FP8X4),
+                        lhsT_scale=w1_scales[:, g, 0, h * P : (h + 1) * P],
+                        rhs=p_codes[sweep * PASSES + g].bitcast(FP8X4),
+                        rhs_scale=p_scales[sweep * PASSES + g],
+                        start=(g == 0),
+                        stop=(g == PASSES - 1),
+                    )
+
+        def best_of_8_points(g):
+            a_grouped[g] = late.tile([P, PACK * VOXELS], BF16, name="a_grouped", align_bytes=64)
+            nc.vector.tensor_tensor(out=a_grouped[g][:], in0=peak[g], in1=peak[PASSES + g], op=ALU.max)
+
+        def quantise_a(g):
+            nc.vector.quantize_mx(out=a_codes[:, g, :].bitcast(FP8X4), scales=a_scales[:, g, :], in_=a_grouped[g][:])
+
+        def is_unit(u):
+            return 0 <= u < UNITS
+
+        for k in range(PASSES, UNITS + 5):
+            if is_unit(k):
+                matmul_and_relu(k)
+            if is_unit(k - 3) and k - 3 >= PASSES:
+                layer1(k - 3 - PASSES)
+            if is_unit(k - 1):
+                regroup(k - 1)
+            if is_unit(k - 2):
+                best_of_2_pairs(k - 2)
+            if is_unit(k - 1):
+                quantise_p(k - 1)
+            if is_unit(k - 2):
+                best_of_4_points(k - 2)
+            if is_unit(k - 3) and k - 3 >= PASSES:
+                best_of_8_points(k - 3 - PASSES)
+            if is_unit(k - 4) and k - 4 >= PASSES:
+                quantise_a(k - 4 - PASSES)
+
+        ya_ps = [psum_y0.tile([P, VOXELS], F32, name="ya_ps%d" % h, tag="y0") for h in range(2)]
+        for g in range(PASSES):
             for h in range(2):
                 nc.tensor.matmul_mx(
-                    out=acc[h][half][:],
-                    lhsT=w1_codes[:, 0, g, h * P : (h + 1) * P].bitcast(FP8X4),
-                    lhsT_scale=w1_scales[:, 0, g, h * P : (h + 1) * P],
-                    rhs=codes.bitcast(FP8X4),
-                    rhs_scale=scales,
-                    start=(g == 0),
-                    stop=(g == PASSES - 1),
-                )
-
-        for group in range(GROUPS):
-            passes = slice(GROUP * group, GROUP * (group + 1))
-            grouped = pairs.tile([P, GROUP, PACK * HALF], BF16, align_bytes=64)
-            for i in range(GROUP):
-                g = GROUP * group + i
-                p_codes = late.tile([P, HALF], U32, align_bytes=64)
-                p_scales = late.tile([P, HALF], U8, align_bytes=64)
-                layer0(g, 1, grouped[:, i, :], p_codes[:], p_scales[:])
-                layer1(g, 0, p_codes_first[:, g, :], p_scales_first[:, g, :])
-                layer1(g, 1, p_codes[:], p_scales[:])
-            peak = late.tile([P, GROUP, PACK * VOXELS], BF16)
-            peak_of_4_points(grouped, peak[:])
-            a_grouped = late.tile([P, GROUP, PACK * VOXELS], BF16, align_bytes=64)
-            nc.vector.tensor_tensor(out=a_grouped[:], in0=peak[:], in1=peak_first[:, passes, :], op=ALU.max)
-            nc.vector.quantize_mx(
-                out=a_codes[:, passes, :].rearrange("p g n -> p (g n)").bitcast(FP8X4),
-                scales=a_scales[:, passes, :].rearrange("p g n -> p (g n)"),
-                in_=a_grouped[:].rearrange("p g w -> p (g w)"),
-            )
-
-        ya = last.tile([P, 2, VOXELS], F32)
-        for h in range(2):
-            ya_ps = psum_y0.tile([P, VOXELS], F32, tag="y0")
-            for g in range(PASSES):
-                nc.tensor.matmul_mx(
-                    out=ya_ps[:],
-                    lhsT=w1_codes[:, 1, g, h * P : (h + 1) * P].bitcast(FP8X4),
-                    lhsT_scale=w1_scales[:, 1, g, h * P : (h + 1) * P],
+                    out=ya_ps[h][:],
+                    lhsT=w1_codes[:, g, 1, h * P : (h + 1) * P].bitcast(FP8X4),
+                    lhsT_scale=w1_scales[:, g, 1, h * P : (h + 1) * P],
                     rhs=a_codes[:, g, :].bitcast(FP8X4),
                     rhs_scale=a_scales[:, g, :],
                     start=(g == 0),
                     stop=(g == PASSES - 1),
                 )
-            nc.scalar.copy(out=ya[:, h, :], in_=ya_ps[:])
+        ya = last.tile([P, 2, VOXELS], F32)
+        for h in range(2):
+            nc.scalar.copy(out=ya[:, h, :], in_=ya_ps[h][:])
 
         y1 = last.tile([P, 2, 2, HALF], F32)
         stats1 = last.tile([P, 2, 2, 6], F32)
         mv1 = last.tile([P, 2, 2], F32)
         for h in range(2):
-            for half in range(2):
+            for sweep in range(2):
                 nc.vector.tensor_tensor(
-                    out=y1[:, h, half, :].rearrange("p (m n) -> p m n", n=VOXELS),
-                    in0=acc[h][half][:].rearrange("p (m n) -> p m n", n=VOXELS),
+                    out=y1[:, h, sweep, :].rearrange("p (m n) -> p m n", n=VOXELS),
+                    in0=acc[h][sweep][:].rearrange("p (m n) -> p m n", n=VOXELS),
                     in1=ya[:, h, :].unsqueeze(1).to_broadcast([P, POINTS // 2, VOXELS]),
                     op=ALU.add,
                 )
-                nc.vector.bn_stats(out=stats1[:, h, half, :], in_=y1[:, h, half, :])
+        for h in range(2):
+            for sweep in range(2):
+                nc.vector.bn_stats(out=stats1[:, h, sweep, :], in_=y1[:, h, sweep, :])
+        for h in range(2):
             nc.vector.bn_aggr(out=mv1[:, h, :], in_=stats1[:, h, :, :].rearrange("p q s -> p (q s)"))
         var_eps1 = last.tile([P, 2], F32)
         std1 = last.tile([P, 2], F32)
@@ -314,6 +406,7 @@ def tile_vfe_k_kernel(tc, voxel_feats, W0, gamma0, beta0, W1, gamma1, beta1, out
                 out=z[:, h, :], in_=y1[:, h, :, :].rearrange("p q r -> p (q r)"), func=ACT.Relu,
                 bias=shift1[:, h : h + 1], scale=scale1[:, h : h + 1],
             )
+        for h in range(2):
             nc.vector.tensor_tensor(out=z4[:, h, :], in0=z[:, h, 0:512], in1=z[:, h, 512:1024], op=ALU.max)
             nc.vector.tensor_tensor(out=z2[:, h, :], in0=z4[:, h, 0:256], in1=z4[:, h, 256:512], op=ALU.max)
             nc.vector.tensor_tensor(out=z1[:, h, :], in0=z2[:, h, 0:128], in1=z2[:, h, 128:256], op=ALU.max)

from contextlib import ExitStack

import concourse.mybir as mybir
from concourse.masks import make_identity

BF16 = mybir.dt.bfloat16
F32 = mybir.dt.float32
U32 = mybir.dt.uint32
U8 = mybir.dt.uint8
FP8X4 = mybir.dt.float8_e4m3fn_x4
ALU = mybir.AluOpType
ACT = mybir.ActivationFunctionType
AX = mybir.AxisListType

P = 128
VOXELS = 128
POINTS = 8
ROWS = VOXELS * POINTS
C = 128
C0 = 8192
C1 = 256
EPS = 1e-3
PACK = 4
K_PASS = P * PACK
PASSES = C0 // K_PASS
CHUNKS = C0 // P
HALF = ROWS // 2
UNITS = 2 * PASSES
LEAD_W0 = 4
LEAD_VAR = 3
LEAD_BN = 2
LEAD_W1 = 4
FETCH = 2

FLOPS = 2 * ROWS * C * C0 + 2 * ROWS * C0 * C1 + 2 * VOXELS * C0 * C1


def tile_vfe_k_kernel(tc, voxel_feats, W0, gamma0, beta0, W1, gamma1, beta1, out):
    nc = tc.nc
    with ExitStack() as ctx:
        ctx.enter_context(tc.manual_schedule())
        keep = ctx.enter_context(tc.tile_pool(name="keep", bufs=1))
        flow = ctx.enter_context(tc.tile_pool(name="flow", bufs=3))
        psum_y0 = ctx.enter_context(tc.psum_pool(name="psum_y0", bufs=3))

        xT = keep.tile([P, ROWS], BF16)
        ident_bf = keep.tile([P, P], BF16)
        ident_f32 = keep.tile([P, P], F32)
        gb = keep.tile([P, 132], F32)
        w0T = keep.tile([P, CHUNKS, P], BF16)
        scale0 = keep.tile([P, CHUNKS], F32)
        shift0 = keep.tile([P, CHUNKS], F32)
        w1_codes = keep.tile([P, PASSES, 2, C1], U32, align_bytes=64)
        w1_scales = keep.tile([P, PASSES, 2, C1], U8, align_bytes=64)
        p_codes_first = keep.tile([P, PASSES, HALF], U32, align_bytes=64)
        p_scales_first = keep.tile([P, PASSES, HALF], U8, align_bytes=64)
        peak_first = keep.tile([P, PASSES, PACK * VOXELS], BF16)
        a_codes = keep.tile([P, PASSES, VOXELS], U32, align_bytes=64)
        a_scales = keep.tile([P, PASSES, VOXELS], U8, align_bytes=64)
        gamma0_t = gb[:, 0:CHUNKS]
        beta0_t = gb[:, CHUNKS : 2 * CHUNKS]
        gamma1_t = gb[:, 128:130]
        beta1_t = gb[:, 130:132]

        planes = {}
        grouped = {}
        best2 = {}
        p_codes = {}
        p_scales = {}
        peak = {}

        def matmul_and_relu(u):
            g, sweep = u % PASSES, u // PASSES
            planes[u] = flow.tile([P, PACK, HALF], BF16, name="planes")
            for t in range(PACK):
                j = PACK * g + t
                y0_ps = psum_y0.tile([P, HALF], F32, tag="y0")
                nc.tensor.matmul(out=y0_ps[:], lhsT=w0T[:, j, :], rhs=xT[:, sweep * HALF : (sweep + 1) * HALF], start=True, stop=True)
                nc.scalar.activation(
                    out=planes[u][:, t, :], in_=y0_ps[:], func=ACT.Relu, bias=shift0[:, j : j + 1], scale=scale0[:, j : j + 1]
                )

        def regroup(u):
            grouped[u] = flow.tile([P, PACK * HALF], BF16, name="grouped", align_bytes=64)
            nc.vector.tensor_copy(
                out=grouped[u][:].rearrange("p (c i t) -> p c t i", i=4, t=PACK),
                in_=planes[u][:].rearrange("p t (c i) -> p c t i", i=4),
            )

        def quantise_p(u):
            g, sweep = u % PASSES, u // PASSES
            if sweep == 0:
                p_codes[u] = p_codes_first[:, g, :]
                p_scales[u] = p_scales_first[:, g, :]
            else:
                p_codes[u] = late.tile([P, HALF], U32, name="p_codes", align_bytes=64)[:]
                p_scales[u] = late.tile([P, HALF], U8, name="p_scales", align_bytes=64)[:]
            nc.vector.quantize_mx(out=p_codes[u].bitcast(FP8X4), scales=p_scales[u], in_=grouped[u][:])

        def best_of_2_pairs(u):
            best2[u] = flow.tile([P, 2 * PACK * VOXELS], BF16, name="best2")
            nc.vector.tensor_tensor(out=best2[u][:], in0=grouped[u][:, 0:1024], in1=grouped[u][:, 1024:2048], op=ALU.max)

        def best_of_4_points(u):
            g, sweep = u % PASSES, u // PASSES
            if sweep == 0:
                peak[u] = peak_first[:, g, :]
            else:
                peak[u] = late.tile([P, PACK * VOXELS], BF16, name="peak")[:]
            nc.vector.tensor_tensor(out=peak[u], in0=best2[u][:, 0:512], in1=best2[u][:, 512:1024], op=ALU.max)

        with ExitStack() as first:
            once = first.enter_context(tc.tile_pool(name="once", bufs=1))
            stage = first.enter_context(tc.tile_pool(name="stage", bufs=2))
            loads = first.enter_context(tc.tile_pool(name="loads", bufs=4))
            psum_two = first.enter_context(tc.psum_pool(name="psum_two", bufs=2))
            psum_one = first.enter_context(tc.psum_pool(name="psum_one", bufs=1))

            x_sb = once.tile([P, POINTS, C], BF16)
            nc.sync.dma_start(out=x_sb[:], in_=voxel_feats)
            gb_rows = once.tile([P, 2 * P], BF16)
            nc.vector.memset(gb_rows[:], 0.0)
            nc.scalar.dma_start(out=gb_rows[0:32, :], in_=gamma0.rearrange("(r w) -> r w", w=2 * P))
            nc.scalar.dma_start(out=gb_rows[32:64, :], in_=beta0.rearrange("(r w) -> r w", w=2 * P))
            nc.scalar.dma_start(out=gb_rows[64:65, :], in_=gamma1.rearrange("(r w) -> r w", w=2 * P))
            nc.scalar.dma_start(out=gb_rows[65:66, :], in_=beta1.rearrange("(r w) -> r w", w=2 * P))
            w0_sb = once.tile([P, CHUNKS, C], BF16)
            w0_view = W0.rearrange("(a p e) c -> p a (e c)", p=P, e=2)
            w0_dst = w0_sb[:].rearrange("p (a e) c -> p a (e c)", e=2)
            for piece in range(4):
                rows = slice(8 * piece, 8 * piece + 8)
                nc.scalar.dma_start(out=w0_dst[:, rows, :], in_=w0_view[:, rows, :])
            w1_view = W1.rearrange("(n h) k -> n h k", h=2)
            w1_raw = {}

            def load_w1(g):
                w1_raw[g] = loads.tile([P, 2, 2, K_PASS], BF16, name="w1_raw")
                for part in range(2):
                    k0 = part * C0 + g * K_PASS
                    nc.sync.dma_start(out=w1_raw[g][:, part, :, :], in_=w1_view[:, :, k0 : k0 + K_PASS])

            for g in range(FETCH):
                load_w1(g)

            make_identity(nc, ident_bf[:])
            make_identity(nc, ident_f32[:])
            ones_bf = once.tile([P, P], BF16)
            nc.vector.memset(ones_bf[:], 1.0)
            eps_col = once.tile([P, 1], F32)
            nc.vector.memset(eps_col[:], 0.0)
            nc.vector.tensor_scalar(out=eps_col[:], in0=eps_col[:], scalar1=EPS, scalar2=None, op0=ALU.add)
            warm = once.tile([P, 1], F32)
            nc.scalar.sqrt(out=warm[:], in_=eps_col[:])

            sum_ps = psum_two.tile([P, C], F32, tag="wcov")
            for m in range(POINTS):
                nc.tensor.matmul(out=sum_ps[:], lhsT=ones_bf[:], rhs=x_sb[:, m, :], start=(m == 0), stop=(m == POINTS - 1))
            col_ps = psum_one.tile([P, 2], F32, tag="mean")
            for m in range(POINTS):
                nc.tensor.matmul(out=col_ps[:], lhsT=x_sb[:, m, :], rhs=ones_bf[:, 0:2], start=(m == 0), stop=(m == POINTS - 1))
            mu_rows = once.tile([P, C], F32)
            nc.vector.tensor_scalar(out=mu_rows[:], in0=sum_ps[:], scalar1=1.0 / ROWS, scalar2=None, op0=ALU.mult)
            xc = once.tile([P, POINTS, C], F32)
            nc.vector.tensor_tensor(
                out=xc[:], in0=x_sb[:], in1=mu_rows[:].unsqueeze(1).to_broadcast([P, POINTS, C]), op=ALU.subtract
            )
            xt_ps = psum_one.tile([P, POINTS, VOXELS], BF16, tag="w0t")
            for m in range(POINTS):
                nc.tensor.transpose(xt_ps[:, m, :], x_sb[:, m, :], ident_bf[:])
            nc.scalar.copy(out=xT[:], in_=xt_ps[:].rearrange("p m n -> p (m n)"))
            gb_ps = psum_one.tile([P, P], F32, tag="w1t")
            nc.tensor.transpose(gb_ps[:], gb_rows[:].bitcast(F32), ident_f32[:])
            cov_ps = psum_two.tile([P, C], F32, tag="wcov")
            for m in range(POINTS):
                nc.tensor.matmul(out=cov_ps[:], lhsT=xc[:, m, :], rhs=xc[:, m, :], start=(m == 0), stop=(m == POINTS - 1))

            mu_pieces = once.tile([P, 4], BF16)
            nc.vector.memset(mu_pieces[:], 0.0)
            rest0 = once.tile([P, 1], F32)
            rest1 = once.tile([P, 1], F32)
            rest2 = once.tile([P, 1], F32)
            nc.vector.tensor_scalar(out=rest0[:], in0=col_ps[:, 0:1], scalar1=1.0 / ROWS, scalar2=None, op0=ALU.mult)
            nc.vector.tensor_copy(out=mu_pieces[:, 0:1], in_=rest0[:])
            nc.vector.tensor_tensor(out=rest1[:], in0=rest0[:], in1=mu_pieces[:, 0:1], op=ALU.subtract)
            nc.vector.tensor_copy(out=mu_pieces[:, 1:2], in_=rest1[:])
            nc.vector.tensor_tensor(out=rest2[:], in0=rest1[:], in1=mu_pieces[:, 1:2], op=ALU.subtract)
            nc.vector.tensor_copy(out=mu_pieces[:, 2:3], in_=rest2[:])
            nc.vector.tensor_copy(out=gb[:], in_=gb_ps[:].bitcast(BF16)[:, 0:132])
            cov = once.tile([P, C], F32)
            nc.vector.tensor_scalar(out=cov[:], in0=cov_ps[:], scalar1=1.0 / ROWS, scalar2=None, op0=ALU.mult)

            var0 = once.tile([P, CHUNKS], F32)
            std0 = once.tile([P, CHUNKS], F32)
            rstd0 = once.tile([P, CHUNKS], F32)
            mean_pieces = once.tile([P, CHUNKS, 4], F32)
            mean_hi = once.tile([P, CHUNKS], F32)
            mean0 = once.tile([P, CHUNKS], F32)
            mscale0 = once.tile([P, CHUNKS], F32)
            w0T_f32 = {}
            wcov_ps = {}
            mean_ps = {}
            prod = {}
            w1_grouped = {}

            def transpose_w0(g):
                chunks = slice(PACK * g, PACK * (g + 1))
                w0t_ps = psum_one.tile([P, PACK, P], BF16, tag="w0t")
                for t in range(PACK):
                    nc.tensor.transpose(w0t_ps[:, t, :], w0_sb[:, PACK * g + t, :], ident_bf[:])
                nc.scalar.copy(out=w0T[:, chunks, :], in_=w0t_ps[:])
                w0T_f32[g] = stage.tile([P, PACK, P], F32, name="w0T_f32")
                nc.gpsimd.tensor_scalar(
                    out=w0T_f32[g][:], in0=w0T[:, chunks, :], scalar1=1.0, scalar2=0.0, op0=ALU.mult, op1=ALU.add
                )

            def w0_times_cov(g):
                wcov_ps[g] = psum_two.tile([P, PACK, C], F32, name="wcov_ps", tag="wcov")
                mean_ps[g] = psum_one.tile([P, PACK, 4], F32, name="mean_ps", tag="mean")
                for t in range(PACK):
                    nc.tensor.matmul(out=wcov_ps[g][:, t, :], lhsT=w0T_f32[g][:, t, :], rhs=cov[:], start=True, stop=True)
                    nc.tensor.matmul(out=mean_ps[g][:, t, :], lhsT=w0T[:, PACK * g + t, :], rhs=mu_pieces[:], start=True, stop=True)

            def save_mean(g):
                nc.scalar.copy(out=mean_pieces[:, PACK * g : PACK * (g + 1), :], in_=mean_ps[g][:])

            def variance_product(g):
                prod[g] = stage.tile([P, PACK, C], F32, name="prod")
                nc.vector.tensor_tensor(out=prod[g][:], in0=wcov_ps[g][:], in1=w0_sb[:, PACK * g : PACK * (g + 1), :], op=ALU.mult)

            def variance_sum(g):
                nc.vector.tensor_reduce(out=var0[:, PACK * g : PACK * (g + 1)], in_=prod[g][:], axis=AX.X, op=ALU.add)

            def standard_deviation(g):
                cols = slice(PACK * g, PACK * (g + 1))
                nc.scalar.activation(out=std0[:, cols], in_=var0[:, cols], func=ACT.Sqrt, bias=eps_col[:, 0:1], scale=1.0)

            def one_over_std(g):
                cols = slice(PACK * g, PACK * (g + 1))
                nc.vector.reciprocal(out=rstd0[:, cols], in_=std0[:, cols])

            def scale_and_shift(g):
                cols = slice(PACK * g, PACK * (g + 1))
                nc.gpsimd.tensor_tensor(out=mean_hi[:, cols], in0=mean_pieces[:, cols, 0], in1=mean_pieces[:, cols, 1], op=ALU.add)
                nc.gpsimd.tensor_tensor(out=mean0[:, cols], in0=mean_hi[:, cols], in1=mean_pieces[:, cols, 2], op=ALU.add)
                nc.gpsimd.tensor_tensor(out=scale0[:, cols], in0=gamma0_t[:, cols], in1=rstd0[:, cols], op=ALU.mult)
                nc.gpsimd.tensor_tensor(out=mscale0[:, cols], in0=mean0[:, cols], in1=scale0[:, cols], op=ALU.mult)
                nc.gpsimd.tensor_tensor(out=shift0[:, cols], in0=beta0_t[:, cols], in1=mscale0[:, cols], op=ALU.subtract)

            def transpose_w1(g, part):
                if part == 0:
                    w1_grouped[g] = stage.tile([P, 2, PACK * C1], BF16, name="w1_grouped", align_bytes=64)
                w1_words = w1_raw[g][:, part, :, :].bitcast(F32)
                w1t_ps = psum_one.tile([P, 2, 2, P], F32, tag="w1t")
                for h in range(2):
                    for u in range(2):
                        nc.tensor.transpose(w1t_ps[:, h, u, :], w1_words[:, h, 128 * u : 128 * (u + 1)], ident_f32[:])
                nc.scalar.copy(
                    out=w1_grouped[g][:, part, :].bitcast(F32).rearrange("p (h n u) -> p h n u", h=2, u=2),
                    in_=w1t_ps[:].rearrange("p h u n -> p h n u"),
                )

            def quantise_w1(g):
                nc.vector.quantize_mx(
                    out=w1_codes[:, g, :, :].rearrange("p s n -> p (s n)").bitcast(FP8X4),
                    scales=w1_scales[:, g, :, :].rearrange("p s n -> p (s n)"),
                    in_=w1_grouped[g][:].rearrange("p s w -> p (s w)"),
                )

            def in_range(g):
                return 0 <= g < PASSES

            for k in range(-LEAD_W0, PASSES):
                if in_range(k + LEAD_W1 + FETCH):
                    load_w1(k + LEAD_W1 + FETCH)
                if in_range(k + LEAD_W0 - 1):
                    save_mean(k + LEAD_W0 - 1)
                if in_range(k + LEAD_BN):
                    standard_deviation(k + LEAD_BN)
                if in_range(k + LEAD_W0):
                    transpose_w0(k + LEAD_W0)
                if in_range(k + LEAD_W1):
                    transpose_w1(k + LEAD_W1, 0)
                if in_range(k):
                    matmul_and_relu(k)
                if in_range(k + LEAD_W1):
                    transpose_w1(k + LEAD_W1, 1)
                if in_range(k + LEAD_W0):
                    w0_times_cov(k + LEAD_W0)
                if in_range(k - 1):
                    regroup(k - 1)
                if in_range(k + LEAD_BN):
                    one_over_std(k + LEAD_BN)
                    scale_and_shift(k + LEAD_BN)
                if in_range(k + LEAD_VAR):
                    variance_product(k + LEAD_VAR)
                if in_range(k - 2):
                    best_of_2_pairs(k - 2)
                if in_range(k - 1):
                    quantise_p(k - 1)
                if in_range(k + LEAD_VAR):
                    variance_sum(k + LEAD_VAR)
                if in_range(k - 2):
                    best_of_4_points(k - 2)
                if in_range(k + LEAD_W1 - 1):
                    quantise_w1(k + LEAD_W1 - 1)

        last = ctx.enter_context(tc.tile_pool(name="last", bufs=1))
        late = ctx.enter_context(tc.tile_pool(name="late", bufs=4))
        psum_acc = ctx.enter_context(tc.psum_pool(name="psum_acc", bufs=1))
        acc = [[psum_acc.tile([P, HALF], F32, name="acc%d%d" % (h, sweep)) for sweep in range(2)] for h in range(2)]
        a_grouped = {}

        def layer1(g):
            for sweep in range(2):
                for h in range(2):
                    nc.tensor.matmul_mx(
                        out=acc[h][sweep][:],
                        lhsT=w1_codes[:, g, 0, h * P : (h + 1) * P].bitcast(FP8X4),
                        lhsT_scale=w1_scales[:, g, 0, h * P : (h + 1) * P],
                        rhs=p_codes[sweep * PASSES + g].bitcast(FP8X4),
                        rhs_scale=p_scales[sweep * PASSES + g],
                        start=(g == 0),
                        stop=(g == PASSES - 1),
                    )

        def best_of_8_points(g):
            a_grouped[g] = late.tile([P, PACK * VOXELS], BF16, name="a_grouped", align_bytes=64)
            nc.vector.tensor_tensor(out=a_grouped[g][:], in0=peak[g], in1=peak[PASSES + g], op=ALU.max)

        def quantise_a(g):
            nc.vector.quantize_mx(out=a_codes[:, g, :].bitcast(FP8X4), scales=a_scales[:, g, :], in_=a_grouped[g][:])

        def is_unit(u):
            return 0 <= u < UNITS

        for k in range(PASSES, UNITS + 5):
            if is_unit(k):
                matmul_and_relu(k)
            if is_unit(k - 3) and k - 3 >= PASSES:
                layer1(k - 3 - PASSES)
            if is_unit(k - 1):
                regroup(k - 1)
            if is_unit(k - 2):
                best_of_2_pairs(k - 2)
            if is_unit(k - 1):
                quantise_p(k - 1)
            if is_unit(k - 2):
                best_of_4_points(k - 2)
            if is_unit(k - 3) and k - 3 >= PASSES:
                best_of_8_points(k - 3 - PASSES)
            if is_unit(k - 4) and k - 4 >= PASSES:
                quantise_a(k - 4 - PASSES)

        ya_ps = [psum_y0.tile([P, VOXELS], F32, name="ya_ps%d" % h, tag="y0") for h in range(2)]
        for g in range(PASSES):
            for h in range(2):
                nc.tensor.matmul_mx(
                    out=ya_ps[h][:],
                    lhsT=w1_codes[:, g, 1, h * P : (h + 1) * P].bitcast(FP8X4),
                    lhsT_scale=w1_scales[:, g, 1, h * P : (h + 1) * P],
                    rhs=a_codes[:, g, :].bitcast(FP8X4),
                    rhs_scale=a_scales[:, g, :],
                    start=(g == 0),
                    stop=(g == PASSES - 1),
                )
        ya = last.tile([P, 2, VOXELS], F32)
        for h in range(2):
            nc.scalar.copy(out=ya[:, h, :], in_=ya_ps[h][:])

        y1 = last.tile([P, 2, 2, HALF], F32)
        stats1 = last.tile([P, 2, 2, 6], F32)
        mv1 = last.tile([P, 2, 2], F32)
        for h in range(2):
            for sweep in range(2):
                nc.vector.tensor_tensor(
                    out=y1[:, h, sweep, :].rearrange("p (m n) -> p m n", n=VOXELS),
                    in0=acc[h][sweep][:].rearrange("p (m n) -> p m n", n=VOXELS),
                    in1=ya[:, h, :].unsqueeze(1).to_broadcast([P, POINTS // 2, VOXELS]),
                    op=ALU.add,
                )
        for h in range(2):
            for sweep in range(2):
                nc.vector.bn_stats(out=stats1[:, h, sweep, :], in_=y1[:, h, sweep, :])
        for h in range(2):
            nc.vector.bn_aggr(out=mv1[:, h, :], in_=stats1[:, h, :, :].rearrange("p q s -> p (q s)"))
        var_eps1 = last.tile([P, 2], F32)
        std1 = last.tile([P, 2], F32)
        rstd1 = last.tile([P, 2], F32)
        scale1 = last.tile([P, 2], F32)
        mscale1 = last.tile([P, 2], F32)
        shift1 = last.tile([P, 2], F32)
        nc.vector.tensor_scalar(out=var_eps1[:], in0=mv1[:, :, 1], scalar1=EPS, scalar2=None, op0=ALU.add)
        nc.scalar.sqrt(out=std1[:], in_=var_eps1[:])
        nc.vector.reciprocal(out=rstd1[:], in_=std1[:])
        nc.vector.tensor_tensor(out=scale1[:], in0=gamma1_t, in1=rstd1[:], op=ALU.mult)
        nc.vector.tensor_tensor(out=mscale1[:], in0=mv1[:, :, 0], in1=scale1[:], op=ALU.mult)
        nc.vector.tensor_tensor(out=shift1[:], in0=beta1_t, in1=mscale1[:], op=ALU.subtract)

        z = last.tile([P, 2, ROWS], F32)
        z4 = last.tile([P, 2, 512], F32)
        z2 = last.tile([P, 2, 256], F32)
        z1 = last.tile([P, 2, VOXELS], F32)
        out_ps = psum_y0.tile([P, 2, P], F32, tag="y0")
        for h in range(2):
            nc.scalar.activation(
                out=z[:, h, :], in_=y1[:, h, :, :].rearrange("p q r -> p (q r)"), func=ACT.Relu,
                bias=shift1[:, h : h + 1], scale=scale1[:, h : h + 1],
            )
        for h in range(2):
            nc.vector.tensor_tensor(out=z4[:, h, :], in0=z[:, h, 0:512], in1=z[:, h, 512:1024], op=ALU.max)
            nc.vector.tensor_tensor(out=z2[:, h, :], in0=z4[:, h, 0:256], in1=z4[:, h, 256:512], op=ALU.max)
            nc.vector.tensor_tensor(out=z1[:, h, :], in0=z2[:, h, 0:128], in1=z2[:, h, 128:256], op=ALU.max)
            nc.tensor.transpose(out_ps[:, h, :], z1[:, h, :], ident_f32[:])
        out_sb = last.tile([P, P, 2], F32)
        nc.vector.tensor_copy(out=out_sb[:], in_=out_ps[:].rearrange("p h c -> p c h"))
        nc.sync.dma_start(out=out, in_=out_sb[:].rearrange("p c h -> p (c h)"))
